import numpy as np
import ml_dtypes


def mxq(x, axis, fmt="e4m3"):
    dtype, down = {"e4m3": (ml_dtypes.float8_e4m3fn, 7), "e5m2": (ml_dtypes.float8_e5m2, 14)}[fmt]
    v = np.moveaxis(np.asarray(x, np.float32).astype(ml_dtypes.bfloat16).astype(np.float64), axis, -1)
    blocks = v.reshape(v.shape[:-1] + (-1, 32))
    amax = np.abs(blocks).max(-1, keepdims=True)
    byte = np.maximum(np.where(amax > 0, np.frexp(amax)[1] - 1 + 127, 0) - down, 1)
    scale = np.exp2(byte - 127.0)
    codes = (blocks / scale).astype(np.float32).astype(dtype).astype(np.float64)
    return np.moveaxis((codes * scale).reshape(v.shape), -1, axis)


WIDE = False


def mx_kscale(k, group=512):
    if not WIDE:
        return np.ones(k)
    levels = np.array([20, -20, 10, -10, 0])
    if group != 512:
        return np.exp2(np.random.permutation(np.resize(levels, k // group))).repeat(group)
    a = np.random.permutation(np.resize(levels, k // 512 * 4)).reshape(k // 512, 4)
    idx = np.arange(k)
    return np.exp2(a[idx // 512, idx % 128 // 32])


BF16 = ml_dtypes.bfloat16


def bf(x):
    return np.asarray(x, np.float32).astype(BF16)


def f64(x):
    return np.asarray(x).astype(np.float64)


B, IN, OUT = 4096, 1024, 512
QI, QO = IN // 4, OUT // 4


def _hamilton_weight(Wr, Wi, Wj, Wk):
    return np.concatenate([
        np.concatenate([Wr, Wi, Wj, Wk], axis=1),
        np.concatenate([-Wi, Wr, Wk, -Wj], axis=1),
        np.concatenate([-Wj, -Wk, Wr, Wi], axis=1),
        np.concatenate([-Wk, Wj, -Wi, Wr], axis=1),
    ], axis=0)


def _hamilton_bias(br, bi, bj, bk):
    return np.concatenate([
        br - bi - bj - bk,
        br + bi + bj - bk,
        br - bi + bj + bk,
        br + bi - bj + bk,
    ], axis=0)


def setup_inputs():
    u = mx_kscale(QO, group=QO // 4)
    c = 1.0 / np.sqrt(QI)
    x = np.random.standard_normal((B, IN))
    Wr = np.random.standard_normal((QI, QO)) * c / u[None, :]
    Wi = np.random.standard_normal((QI, QO)) * c / u[None, :]
    Wj = np.random.standard_normal((QI, QO)) * c / u[None, :]
    Wk = np.random.standard_normal((QI, QO)) * c / u[None, :]
    br = np.random.standard_normal(QO) * 0.3
    bi = np.random.standard_normal(QO) * 0.3
    bj = np.random.standard_normal(QO) * 0.3
    bk = np.random.standard_normal(QO) * 0.3
    g = np.random.standard_normal((B, OUT)) * np.exp2(np.random.randint(-12, 1, (B, 1))) * 4.0 * np.tile(u, 4)[None, :]
    return {"x": bf(x), "Wr": bf(Wr), "Wi": bf(Wi), "Wj": bf(Wj), "Wk": bf(Wk),
            "br": bf(br), "bi": bf(bi), "bj": bf(bj), "bk": bf(bk), "grad_out": bf(g)}


def reference(x, Wr, Wi, Wj, Wk, br, bi, bj, bk, grad_out):
    Wq = mxq(np.concatenate([f64(Wr), f64(Wi), f64(Wj), f64(Wk)], axis=1), 1, "e4m3")
    W = _hamilton_weight(Wq[:, :QO], Wq[:, QO:2 * QO], Wq[:, 2 * QO:3 * QO], Wq[:, 3 * QO:])
    return mxq(f64(grad_out), 1, "e5m2") @ W.T

@@ -1,0 +1,175 @@
+import concourse.mybir as mybir
+from concourse.masks import make_identity
+
+F32 = mybir.dt.float32
+BF16 = mybir.dt.bfloat16
+U32 = mybir.dt.uint32
+U8 = mybir.dt.uint8
+E4M3_X4 = mybir.dt.float8_e4m3fn_x4
+E5M2_X4 = mybir.dt.float8_e5m2_x4
+
+P = 128
+PACK = 4
+K = P * PACK
+N_PASS = 512
+
+TOKENS, IN_FEATURES, OUT_FEATURES = 4096, 1024, 512
+assert OUT_FEATURES == K
+
+TOKEN_TILES = TOKENS // P
+PAIR = 2
+GROUP = 4
+CHUNK = 8
+WORDS = K // 2
+
+HAMILTON = (
+    ((+1.0, 0), (+1.0, 1), (+1.0, 2), (+1.0, 3)),
+    ((-1.0, 1), (+1.0, 0), (+1.0, 3), (-1.0, 2)),
+    ((-1.0, 2), (-1.0, 3), (+1.0, 0), (+1.0, 1)),
+    ((-1.0, 3), (+1.0, 2), (-1.0, 1), (+1.0, 0)),
+)
+BLOCK_ROWS = 4
+BLOCK_K = OUT_FEATURES // 4
+HALVES = IN_FEATURES // 4 // P
+assert HALVES == PAIR
+
+FLOPS = 2 * TOKENS * IN_FEATURES * OUT_FEATURES
+BYTES = 2 * TOKENS * OUT_FEATURES + 2 * IN_FEATURES * BLOCK_K + 4 * TOKENS * IN_FEATURES
+
+
+def pair_to_k_major(nc, banks, identity, row_words, grouped_words):
+    bank = banks.tile([P, PAIR, 2, P], F32)
+    for r in range(PAIR):
+        for u in range(2):
+            nc.tensor.transpose(bank[:, r, u, :], row_words[:, r, u, :], identity)
+    nc.vector.tensor_copy(out=grouped_words, in_=bank[:].rearrange("p r u n -> p r n u"))
+
+
+def tile_quaternionlinear_t_kernel(
+    tc, x, Wr, Wi, Wj, Wk, br, bi, bj, bk, grad_out, out
+):
+    nc = tc.nc
+    g_dram = grad_out.rearrange("(p i) k -> p (i k)", i=TOKEN_TILES)
+    out_dram = out.rearrange("(p i) n -> p (i n)", i=TOKEN_TILES)
+
+    with (
+        tc.tile_pool(name="constants", bufs=1) as constants,
+        tc.tile_pool(name="loads", bufs=TOKEN_TILES // CHUNK) as loads,
+        tc.tile_pool(name="operands", bufs=3) as operands,
+        tc.tile_pool(name="results", bufs=6) as results,
+        tc.psum_pool(name="banks", bufs=2) as banks,
+        tc.psum_pool(name="sums", bufs=6) as sums,
+    ):
+        w_rows = constants.tile([P, BLOCK_ROWS * PAIR * K], BF16)
+        w_blocks = w_rows[:].rearrange(
+            "n (c h j k) -> n c h j k", c=BLOCK_ROWS, h=PAIR, j=4
+        )
+        for m, matrix in enumerate((Wr, Wi, Wj, Wk)):
+            nc.sync.dma_start(
+                out=w_blocks[:, 0, :, m, :],
+                in_=matrix.rearrange("(h n) k -> n h k", n=P),
+            )
+        g_chunks = []
+        for d in range(TOKEN_TILES // CHUNK):
+            g_rows = loads.tile([P, CHUNK * K], BF16)
+            nc.sync.dma_start(
+                out=g_rows[:], in_=g_dram[:, d * CHUNK * K : (d + 1) * CHUNK * K]
+            )
+            g_chunks.append(g_rows)
+
+        identity = constants.tile([P, P], F32)
+        make_identity(nc, identity[:])
+
+        w_grouped = constants.tile([P, IN_FEATURES * PACK], BF16, align_bytes=64)
+        w_codes = constants.tile([P, IN_FEATURES], U32, align_bytes=64)
+        w_scales = constants.tile([P, IN_FEATURES], U8, align_bytes=64)
+        w_row_words = w_rows[:].bitcast(F32).rearrange(
+            "n (c h p u) -> n c h u p", c=BLOCK_ROWS, h=PAIR, u=2
+        )
+        w_grouped_words = w_grouped[:].bitcast(F32).rearrange(
+            "p (c h n u) -> p c h n u", c=BLOCK_ROWS, h=PAIR, u=2
+        )
+        for c in range(BLOCK_ROWS):
+            if c > 0:
+                for j, (sign, m) in enumerate(HAMILTON[c]):
+                    nc.vector.tensor_scalar_mul(
+                        out=w_blocks[:, c, :, j, :],
+                        in0=w_blocks[:, 0, :, m, :],
+                        scalar1=sign,
+                    )
+            pair_to_k_major(
+                nc, banks, identity[:], w_row_words[:, c], w_grouped_words[:, c]
+            )
+        for half in range(IN_FEATURES // N_PASS):
+            cols = slice(half * N_PASS, (half + 1) * N_PASS)
+            nc.vector.quantize_mx(
+                out=w_codes[:, cols].bitcast(E4M3_X4),
+                scales=w_scales[:, cols],
+                in_=w_grouped[:, half * N_PASS * PACK : (half + 1) * N_PASS * PACK],
+            )
+
+        def regroup(s):
+            g_rows = g_chunks[s * GROUP // CHUNK]
+            g_row_words = g_rows[:].bitcast(F32).rearrange(
+                "n (i p u) -> n i u p", i=CHUNK, u=2
+            )
+            g_grouped = operands.tile([P, GROUP * P * PACK], BF16, align_bytes=64)
+            g_grouped_words = g_grouped[:].bitcast(F32).rearrange(
+                "p (i n u) -> p i n u", i=GROUP, u=2
+            )
+            first = s * GROUP % CHUNK
+            for a in range(0, GROUP, PAIR):
+                pair_to_k_major(
+                    nc,
+                    banks,
+                    identity[:],
+                    g_row_words[:, first + a : first + a + PAIR],
+                    g_grouped_words[:, a : a + PAIR],
+                )
+            return g_grouped
+
+        def quantise(g_grouped):
+            g_codes = operands.tile([P, GROUP * P], U32, align_bytes=64)
+            g_scales = operands.tile([P, GROUP * P], U8, align_bytes=64)
+            nc.vector.quantize_mx(
+                out=g_codes[:].bitcast(E5M2_X4), scales=g_scales[:], in_=g_grouped[:]
+            )
+            return g_codes, g_scales
+
+        def multiply(s, g_codes, g_scales):
+            for a in range(0, GROUP, PAIR):
+                out_rows = results.tile([P, PAIR * IN_FEATURES], F32)
+                for r in range(PAIR):
+                    tokens = slice((a + r) * P, (a + r + 1) * P)
+                    for half in range(IN_FEATURES // N_PASS):
+                        cols = slice(half * N_PASS, (half + 1) * N_PASS)
+                        acc = sums.tile([P, N_PASS], F32)
+                        nc.tensor.matmul_mx(
+                            out=acc[:],
+                            lhsT=g_codes[:, tokens].bitcast(E5M2_X4),
+                            lhsT_scale=g_scales[:, tokens],
+                            rhs=w_codes[:, cols].bitcast(E4M3_X4),
+                            rhs_scale=w_scales[:, cols],
+                            start=True,
+                            stop=True,
+                        )
+                        place = out_rows[
+                            :, r * IN_FEATURES + half * N_PASS : r * IN_FEATURES + (half + 1) * N_PASS
+                        ]
+                        if r == PAIR - 1 and half == 1:
+                            nc.vector.tensor_copy(out=place, in_=acc[:])
+                        else:
+                            nc.scalar.copy(out=place, in_=acc[:])
+                first = (s * GROUP + a) * IN_FEATURES
+                nc.sync.dma_start(
+                    out=out_dram[:, first : first + PAIR * IN_FEATURES], in_=out_rows[:]
+                )
+
+        groups = TOKEN_TILES // GROUP
+        g_codes, g_scales = quantise(regroup(0))
+        for s in range(groups):
+            if s + 1 < groups:
+                g_grouped = regroup(s + 1)
+            multiply(s, g_codes, g_scales)
+            if s + 1 < groups:
+                g_codes, g_scales = quantise(g_grouped)

@@ -18,7 +18,6 @@ assert OUT_FEATURES == K
 
 TOKEN_TILES = TOKENS // P
 PAIR = 2
-GROUP = 4
 CHUNK = 8
 WORDS = K // 2
 
@@ -42,7 +41,7 @@ def pair_to_k_major(nc, banks, identity, row_words, grouped_words):
     for r in range(PAIR):
         for u in range(2):
             nc.tensor.transpose(bank[:, r, u, :], row_words[:, r, u, :], identity)
-    nc.vector.tensor_copy(out=grouped_words, in_=bank[:].rearrange("p r u n -> p r n u"))
+    nc.scalar.copy(out=grouped_words, in_=bank[:].rearrange("p r u n -> p r n u"))
 
 
 def tile_quaternionlinear_t_kernel(
@@ -56,7 +55,7 @@ def tile_quaternionlinear_t_kernel(
         tc.tile_pool(name="constants", bufs=1) as constants,
         tc.tile_pool(name="loads", bufs=TOKEN_TILES // CHUNK) as loads,
         tc.tile_pool(name="operands", bufs=3) as operands,
-        tc.tile_pool(name="results", bufs=6) as results,
+        tc.tile_pool(name="results", bufs=8) as results,
         tc.psum_pool(name="banks", bufs=2) as banks,
         tc.psum_pool(name="sums", bufs=6) as sums,
     ):
@@ -100,76 +99,68 @@ def tile_quaternionlinear_t_kernel(
             pair_to_k_major(
                 nc, banks, identity[:], w_row_words[:, c], w_grouped_words[:, c]
             )
-        for half in range(IN_FEATURES // N_PASS):
-            cols = slice(half * N_PASS, (half + 1) * N_PASS)
+            rows = slice(c * PAIR * P, (c + 1) * PAIR * P)
             nc.vector.quantize_mx(
-                out=w_codes[:, cols].bitcast(E4M3_X4),
-                scales=w_scales[:, cols],
-                in_=w_grouped[:, half * N_PASS * PACK : (half + 1) * N_PASS * PACK],
+                out=w_codes[:, rows].bitcast(E4M3_X4),
+                scales=w_scales[:, rows],
+                in_=w_grouped[:, c * PAIR * P * PACK : (c + 1) * PAIR * P * PACK],
             )
 
         def regroup(s):
-            g_rows = g_chunks[s * GROUP // CHUNK]
-            g_row_words = g_rows[:].bitcast(F32).rearrange(
+            g_row_words = g_chunks[s * PAIR // CHUNK][:].bitcast(F32).rearrange(
                 "n (i p u) -> n i u p", i=CHUNK, u=2
             )
-            g_grouped = operands.tile([P, GROUP * P * PACK], BF16, align_bytes=64)
-            g_grouped_words = g_grouped[:].bitcast(F32).rearrange(
-                "p (i n u) -> p i n u", i=GROUP, u=2
+            first = s * PAIR % CHUNK
+            g_grouped = operands.tile([P, PAIR * P * PACK], BF16, align_bytes=64)
+            pair_to_k_major(
+                nc,
+                banks,
+                identity[:],
+                g_row_words[:, first : first + PAIR],
+                g_grouped[:].bitcast(F32).rearrange("p (r n u) -> p r n u", r=PAIR, u=2),
             )
-            first = s * GROUP % CHUNK
-            for a in range(0, GROUP, PAIR):
-                pair_to_k_major(
-                    nc,
-                    banks,
-                    identity[:],
-                    g_row_words[:, first + a : first + a + PAIR],
-                    g_grouped_words[:, a : a + PAIR],
-                )
             return g_grouped
 
         def quantise(g_grouped):
-            g_codes = operands.tile([P, GROUP * P], U32, align_bytes=64)
-            g_scales = operands.tile([P, GROUP * P], U8, align_bytes=64)
+            g_codes = operands.tile([P, PAIR * P], U32, align_bytes=64)
+            g_scales = operands.tile([P, PAIR * P], U8, align_bytes=64)
             nc.vector.quantize_mx(
                 out=g_codes[:].bitcast(E5M2_X4), scales=g_scales[:], in_=g_grouped[:]
             )
             return g_codes, g_scales
 
         def multiply(s, g_codes, g_scales):
-            for a in range(0, GROUP, PAIR):
-                out_rows = results.tile([P, PAIR * IN_FEATURES], F32)
-                for r in range(PAIR):
-                    tokens = slice((a + r) * P, (a + r + 1) * P)
-                    for half in range(IN_FEATURES // N_PASS):
-                        cols = slice(half * N_PASS, (half + 1) * N_PASS)
-                        acc = sums.tile([P, N_PASS], F32)
-                        nc.tensor.matmul_mx(
-                            out=acc[:],
-                            lhsT=g_codes[:, tokens].bitcast(E5M2_X4),
-                            lhsT_scale=g_scales[:, tokens],
-                            rhs=w_codes[:, cols].bitcast(E4M3_X4),
-                            rhs_scale=w_scales[:, cols],
-                            start=True,
-                            stop=True,
-                        )
-                        place = out_rows[
-                            :, r * IN_FEATURES + half * N_PASS : r * IN_FEATURES + (half + 1) * N_PASS
-                        ]
-                        if r == PAIR - 1 and half == 1:
-                            nc.vector.tensor_copy(out=place, in_=acc[:])
-                        else:
-                            nc.scalar.copy(out=place, in_=acc[:])
-                first = (s * GROUP + a) * IN_FEATURES
-                nc.sync.dma_start(
-                    out=out_dram[:, first : first + PAIR * IN_FEATURES], in_=out_rows[:]
-                )
+            out_rows = results.tile([P, PAIR * IN_FEATURES], F32)
+            for r in range(PAIR):
+                tokens = slice(r * P, (r + 1) * P)
+                for half in range(IN_FEATURES // N_PASS):
+                    cols = slice(half * N_PASS, (half + 1) * N_PASS)
+                    acc = sums.tile([P, N_PASS], F32)
+                    nc.tensor.matmul_mx(
+                        out=acc[:],
+                        lhsT=g_codes[:, tokens].bitcast(E5M2_X4),
+                        lhsT_scale=g_scales[:, tokens],
+                        rhs=w_codes[:, cols].bitcast(E4M3_X4),
+                        rhs_scale=w_scales[:, cols],
+                        start=True,
+                        stop=True,
+                    )
+                    first = r * IN_FEATURES + half * N_PASS
+                    place = out_rows[:, first : first + N_PASS]
+                    if half == 0:
+                        nc.scalar.copy(out=place, in_=acc[:])
+                    else:
+                        nc.vector.tensor_copy(out=place, in_=acc[:])
+            first = s * PAIR * IN_FEATURES
+            nc.sync.dma_start(
+                out=out_dram[:, first : first + PAIR * IN_FEATURES], in_=out_rows[:]
+            )
 
-        groups = TOKEN_TILES // GROUP
+        pairs = TOKEN_TILES // PAIR
         g_codes, g_scales = quantise(regroup(0))
-        for s in range(groups):
-            if s + 1 < groups:
+        for s in range(pairs):
+            if s + 1 < pairs:
                 g_grouped = regroup(s + 1)
             multiply(s, g_codes, g_scales)
-            if s + 1 < groups:
+            if s + 1 < pairs:
                 g_codes, g_scales = quantise(g_grouped)

@@ -18,7 +18,8 @@ assert OUT_FEATURES == K
 
 TOKEN_TILES = TOKENS // P
 PAIR = 2
-CHUNK = 8
+CHUNKS = (2, 2, 4, 8, 8, 8)
+assert sum(CHUNKS) == TOKEN_TILES and all(size % PAIR == 0 for size in CHUNKS)
 WORDS = K // 2
 
 HAMILTON = (
@@ -53,7 +54,7 @@ def tile_quaternionlinear_t_kernel(
 
     with (
         tc.tile_pool(name="constants", bufs=1) as constants,
-        tc.tile_pool(name="loads", bufs=TOKEN_TILES // CHUNK) as loads,
+        tc.tile_pool(name="loads", bufs=1) as loads,
         tc.tile_pool(name="operands", bufs=3) as operands,
         tc.tile_pool(name="results", bufs=8) as results,
         tc.psum_pool(name="banks", bufs=2) as banks,
@@ -63,18 +64,22 @@ def tile_quaternionlinear_t_kernel(
         w_blocks = w_rows[:].rearrange(
             "n (c h j k) -> n c h j k", c=BLOCK_ROWS, h=PAIR, j=4
         )
-        for m, matrix in enumerate((Wr, Wi, Wj, Wk)):
-            nc.sync.dma_start(
-                out=w_blocks[:, 0, :, m, :],
-                in_=matrix.rearrange("(h n) k -> n h k", n=P),
+        g_pairs = []
+        for d, size in enumerate(CHUNKS):
+            g_rows = loads.tile([P, size * K], BF16, name="g_rows%d" % d)
+            first = len(g_pairs) * PAIR * K
+            nc.sync.dma_start(out=g_rows[:], in_=g_dram[:, first : first + size * K])
+            g_row_words = g_rows[:].bitcast(F32).rearrange(
+                "n (i p u) -> n i u p", i=size, u=2
             )
-        g_chunks = []
-        for d in range(TOKEN_TILES // CHUNK):
-            g_rows = loads.tile([P, CHUNK * K], BF16)
-            nc.sync.dma_start(
-                out=g_rows[:], in_=g_dram[:, d * CHUNK * K : (d + 1) * CHUNK * K]
-            )
-            g_chunks.append(g_rows)
+            for i in range(0, size, PAIR):
+                g_pairs.append(g_row_words[:, i : i + PAIR])
+            if d == 0:
+                for m, matrix in enumerate((Wr, Wi, Wj, Wk)):
+                    nc.sync.dma_start(
+                        out=w_blocks[:, 0, :, m, :],
+                        in_=matrix.rearrange("(h n) k -> n h k", n=P),
+                    )
 
         identity = constants.tile([P, P], F32)
         make_identity(nc, identity[:])
@@ -88,7 +93,8 @@ def tile_quaternionlinear_t_kernel(
         w_grouped_words = w_grouped[:].bitcast(F32).rearrange(
             "p (c h n u) -> p c h n u", c=BLOCK_ROWS, h=PAIR, u=2
         )
-        for c in range(BLOCK_ROWS):
+
+        def prepare_w(c):
             if c > 0:
                 for j, (sign, m) in enumerate(HAMILTON[c]):
                     nc.vector.tensor_scalar_mul(
@@ -107,16 +113,12 @@ def tile_quaternionlinear_t_kernel(
             )
 
         def regroup(s):
-            g_row_words = g_chunks[s * PAIR // CHUNK][:].bitcast(F32).rearrange(
-                "n (i p u) -> n i u p", i=CHUNK, u=2
-            )
-            first = s * PAIR % CHUNK
             g_grouped = operands.tile([P, PAIR * P * PACK], BF16, align_bytes=64)
             pair_to_k_major(
                 nc,
                 banks,
                 identity[:],
-                g_row_words[:, first : first + PAIR],
+                g_pairs[s],
                 g_grouped[:].bitcast(F32).rearrange("p (r n u) -> p r n u", r=PAIR, u=2),
             )
             return g_grouped
@@ -151,13 +153,20 @@ def tile_quaternionlinear_t_kernel(
                         nc.scalar.copy(out=place, in_=acc[:])
                     else:
                         nc.vector.tensor_copy(out=place, in_=acc[:])
-            first = s * PAIR * IN_FEATURES
-            nc.sync.dma_start(
-                out=out_dram[:, first : first + PAIR * IN_FEATURES], in_=out_rows[:]
-            )
+            pieces = PAIR if s == 0 else 1
+            width = PAIR * IN_FEATURES // pieces
+            for piece in range(pieces):
+                first = s * PAIR * IN_FEATURES + piece * width
+                nc.sync.dma_start(
+                    out=out_dram[:, first : first + width],
+                    in_=out_rows[:, piece * width : (piece + 1) * width],
+                )
 
         pairs = TOKEN_TILES // PAIR
-        g_codes, g_scales = quantise(regroup(0))
+        g_grouped = regroup(0)
+        for c in range(BLOCK_ROWS):
+            prepare_w(c)
+        g_codes, g_scales = quantise(g_grouped)
         for s in range(pairs):
             if s + 1 < pairs:
                 g_grouped = regroup(s + 1)

@@ -163,13 +163,14 @@ def tile_quaternionlinear_t_kernel(
                 )
 
         pairs = TOKEN_TILES // PAIR
-        g_grouped = regroup(0)
+        grouped = {0: regroup(0)}
         for c in range(BLOCK_ROWS):
             prepare_w(c)
-        g_codes, g_scales = quantise(g_grouped)
+        quantised = {0: quantise(grouped[0])}
+        grouped[1] = regroup(1)
         for s in range(pairs):
+            if s + 2 < pairs:
+                grouped[s + 2] = regroup(s + 2)
             if s + 1 < pairs:
-                g_grouped = regroup(s + 1)
-            multiply(s, g_codes, g_scales)
-            if s + 1 < pairs:
-                g_codes, g_scales = quantise(g_grouped)
+                quantised[s + 1] = quantise(grouped[s + 1])
+            multiply(s, quantised[s][0], quantised[s][1])

@@ -17,9 +17,11 @@ TOKENS, IN_FEATURES, OUT_FEATURES = 4096, 1024, 512
 assert OUT_FEATURES == K
 
 TOKEN_TILES = TOKENS // P
+SPAN_TILES = 8
 PAIR = 2
 CHUNKS = (2, 2, 4, 8, 8, 8)
 assert sum(CHUNKS) == TOKEN_TILES and all(size % PAIR == 0 for size in CHUNKS)
+assert sum(CHUNKS[:3]) == SPAN_TILES and all(size == SPAN_TILES for size in CHUNKS[3:])
 WORDS = K // 2
 
 HAMILTON = (
@@ -49,13 +51,13 @@ def tile_quaternionlinear_t_kernel(
     tc, x, Wr, Wi, Wj, Wk, br, bi, bj, bk, grad_out, out
 ):
     nc = tc.nc
-    g_dram = grad_out.rearrange("(p i) k -> p (i k)", i=TOKEN_TILES)
-    out_dram = out.rearrange("(p i) n -> p (i n)", i=TOKEN_TILES)
+    g_dram = grad_out.rearrange("(b p i) k -> b p (i k)", p=P, i=SPAN_TILES)
+    out_dram = out.rearrange("(b p i) n -> b p (i n)", p=P, i=SPAN_TILES)
 
     with (
         tc.tile_pool(name="constants", bufs=1) as constants,
         tc.tile_pool(name="loads", bufs=1) as loads,
-        tc.tile_pool(name="operands", bufs=3) as operands,
+        tc.tile_pool(name="operands", bufs=4) as operands,
         tc.tile_pool(name="results", bufs=8) as results,
         tc.psum_pool(name="banks", bufs=2) as banks,
         tc.psum_pool(name="sums", bufs=6) as sums,
@@ -67,8 +69,10 @@ def tile_quaternionlinear_t_kernel(
         g_pairs = []
         for d, size in enumerate(CHUNKS):
             g_rows = loads.tile([P, size * K], BF16, name="g_rows%d" % d)
-            first = len(g_pairs) * PAIR * K
-            nc.sync.dma_start(out=g_rows[:], in_=g_dram[:, first : first + size * K])
+            span, tile = divmod(len(g_pairs) * PAIR, SPAN_TILES)
+            nc.sync.dma_start(
+                out=g_rows[:], in_=g_dram[span, :, tile * K : (tile + size) * K]
+            )
             g_row_words = g_rows[:].bitcast(F32).rearrange(
                 "n (i p u) -> n i u p", i=size, u=2
             )
@@ -155,10 +159,11 @@ def tile_quaternionlinear_t_kernel(
                         nc.vector.tensor_copy(out=place, in_=acc[:])
             pieces = PAIR if s == 0 else 1
             width = PAIR * IN_FEATURES // pieces
+            span, tile = divmod(s * PAIR, SPAN_TILES)
             for piece in range(pieces):
-                first = s * PAIR * IN_FEATURES + piece * width
+                first = tile * IN_FEATURES + piece * width
                 nc.sync.dma_start(
-                    out=out_dram[:, first : first + width],
+                    out=out_dram[span, :, first : first + width],
                     in_=out_rows[:, piece * width : (piece + 1) * width],
                 )
 
@@ -169,8 +174,10 @@ def tile_quaternionlinear_t_kernel(
         quantised = {0: quantise(grouped[0])}
         grouped[1] = regroup(1)
         for s in range(pairs):
-            if s + 2 < pairs:
-                grouped[s + 2] = regroup(s + 2)
             if s + 1 < pairs:
                 quantised[s + 1] = quantise(grouped[s + 1])
             multiply(s, quantised[s][0], quantised[s][1])
+            if s == 0:
+                grouped[2] = regroup(2)
+            if s + 3 < pairs:
+                grouped[s + 3] = regroup(s + 3)

@@ -23,6 +23,7 @@ CHUNKS = (2, 2, 4, 8, 8, 8)
 assert sum(CHUNKS) == TOKEN_TILES and all(size % PAIR == 0 for size in CHUNKS)
 assert sum(CHUNKS[:3]) == SPAN_TILES and all(size == SPAN_TILES for size in CHUNKS[3:])
 WORDS = K // 2
+WARM_UP = 5
 
 HAMILTON = (
     ((+1.0, 0), (+1.0, 1), (+1.0, 2), (+1.0, 3)),
@@ -88,6 +89,16 @@ def tile_quaternionlinear_t_kernel(
         identity = constants.tile([P, P], F32)
         make_identity(nc, identity[:])
 
+        zeros = constants.tile([P, N_PASS], BF16)
+        nc.vector.memset(zeros[:], 0.0)
+        idle_sum = sums.tile([P, N_PASS], F32, tag="acc")
+
+        def idle_matmuls(count):
+            for w in range(count):
+                nc.tensor.matmul(
+                    out=idle_sum[:], lhsT=zeros[:, :P], rhs=zeros[:], start=True, stop=True
+                )
+
         w_grouped = constants.tile([P, IN_FEATURES * PACK], BF16, align_bytes=64)
         w_codes = constants.tile([P, IN_FEATURES], U32, align_bytes=64)
         w_scales = constants.tile([P, IN_FEATURES], U8, align_bytes=64)
@@ -141,7 +152,7 @@ def tile_quaternionlinear_t_kernel(
                 tokens = slice(r * P, (r + 1) * P)
                 for half in range(IN_FEATURES // N_PASS):
                     cols = slice(half * N_PASS, (half + 1) * N_PASS)
-                    acc = sums.tile([P, N_PASS], F32)
+                    acc = sums.tile([P, N_PASS], F32, tag="acc")
                     nc.tensor.matmul_mx(
                         out=acc[:],
                         lhsT=g_codes[:, tokens].bitcast(E5M2_X4),
@@ -168,11 +179,15 @@ def tile_quaternionlinear_t_kernel(
                 )
 
         pairs = TOKEN_TILES // PAIR
-        grouped = {0: regroup(0)}
-        for c in range(BLOCK_ROWS):
-            prepare_w(c)
-        quantised = {0: quantise(grouped[0])}
-        grouped[1] = regroup(1)
+        with tc.manual_schedule(engines={mybir.EngineType.PE}):
+            idle_matmuls(WARM_UP)
+            grouped = {0: regroup(0)}
+            idle_matmuls(1)
+            for c in range(BLOCK_ROWS):
+                prepare_w(c)
+                idle_matmuls(1)
+            quantised = {0: quantise(grouped[0])}
+            grouped[1] = regroup(1)
         for s in range(pairs):
             if s + 1 < pairs:
                 quantised[s + 1] = quantise(grouped[s + 1])

@@ -23,7 +23,8 @@ CHUNKS = (2, 2, 4, 8, 8, 8)
 assert sum(CHUNKS) == TOKEN_TILES and all(size % PAIR == 0 for size in CHUNKS)
 assert sum(CHUNKS[:3]) == SPAN_TILES and all(size == SPAN_TILES for size in CHUNKS[3:])
 WORDS = K // 2
-WARM_UP = 5
+WARM_UP = 20
+KEEP_WARM = 4
 
 HAMILTON = (
     ((+1.0, 0), (+1.0, 1), (+1.0, 2), (+1.0, 3)),
@@ -86,17 +87,17 @@ def tile_quaternionlinear_t_kernel(
                         in_=matrix.rearrange("(h n) k -> n h k", n=P),
                     )
 
+        zeros = constants.tile([P, P], BF16)
+        nc.gpsimd.memset(zeros[:], 0.0)
         identity = constants.tile([P, P], F32)
         make_identity(nc, identity[:])
 
-        zeros = constants.tile([P, N_PASS], BF16)
-        nc.vector.memset(zeros[:], 0.0)
         idle_sum = sums.tile([P, N_PASS], F32, tag="acc")
 
         def idle_matmuls(count):
             for w in range(count):
                 nc.tensor.matmul(
-                    out=idle_sum[:], lhsT=zeros[:, :P], rhs=zeros[:], start=True, stop=True
+                    out=idle_sum[:, :P], lhsT=zeros[:], rhs=zeros[:], start=True, stop=True
                 )
 
         w_grouped = constants.tile([P, IN_FEATURES * PACK], BF16, align_bytes=64)
@@ -182,10 +183,10 @@ def tile_quaternionlinear_t_kernel(
         with tc.manual_schedule(engines={mybir.EngineType.PE}):
             idle_matmuls(WARM_UP)
             grouped = {0: regroup(0)}
-            idle_matmuls(1)
+            idle_matmuls(KEEP_WARM)
             for c in range(BLOCK_ROWS):
                 prepare_w(c)
-                idle_matmuls(1)
+                idle_matmuls(KEEP_WARM)
             quantised = {0: quantise(grouped[0])}
             grouped[1] = regroup(1)
         for s in range(pairs):

@@ -147,37 +147,45 @@ def tile_quaternionlinear_t_kernel(
             )
             return g_codes, g_scales
 
-        def multiply(s, g_codes, g_scales):
-            out_rows = results.tile([P, PAIR * IN_FEATURES], F32)
+        def one_pass(out_rows, operand, r, half, on_vector):
+            g_codes, g_scales = operand
+            tokens = slice(r * P, (r + 1) * P)
+            cols = slice(half * N_PASS, (half + 1) * N_PASS)
+            acc = sums.tile([P, N_PASS], F32, tag="acc")
+            nc.tensor.matmul_mx(
+                out=acc[:],
+                lhsT=g_codes[:, tokens].bitcast(E5M2_X4),
+                lhsT_scale=g_scales[:, tokens],
+                rhs=w_codes[:, cols].bitcast(E4M3_X4),
+                rhs_scale=w_scales[:, cols],
+                start=True,
+                stop=True,
+            )
+            first = r * IN_FEATURES + half * N_PASS
+            if on_vector:
+                nc.vector.tensor_copy(out=out_rows[:, first : first + N_PASS], in_=acc[:])
+            else:
+                nc.scalar.copy(out=out_rows[:, first : first + N_PASS], in_=acc[:])
+
+        def multiply(s, operand):
+            out_rows = results.tile([P, PAIR * IN_FEATURES], F32, tag="out_rows")
             for r in range(PAIR):
-                tokens = slice(r * P, (r + 1) * P)
                 for half in range(IN_FEATURES // N_PASS):
-                    cols = slice(half * N_PASS, (half + 1) * N_PASS)
-                    acc = sums.tile([P, N_PASS], F32, tag="acc")
-                    nc.tensor.matmul_mx(
-                        out=acc[:],
-                        lhsT=g_codes[:, tokens].bitcast(E5M2_X4),
-                        lhsT_scale=g_scales[:, tokens],
-                        rhs=w_codes[:, cols].bitcast(E4M3_X4),
-                        rhs_scale=w_scales[:, cols],
-                        start=True,
-                        stop=True,
-                    )
-                    first = r * IN_FEATURES + half * N_PASS
-                    place = out_rows[:, first : first + N_PASS]
-                    if half == 0:
-                        nc.scalar.copy(out=place, in_=acc[:])
-                    else:
-                        nc.vector.tensor_copy(out=place, in_=acc[:])
-            pieces = PAIR if s == 0 else 1
-            width = PAIR * IN_FEATURES // pieces
+                    one_pass(out_rows, operand, r, half, on_vector=(half == 1))
             span, tile = divmod(s * PAIR, SPAN_TILES)
-            for piece in range(pieces):
-                first = tile * IN_FEATURES + piece * width
-                nc.sync.dma_start(
-                    out=out_dram[span, :, first : first + width],
-                    in_=out_rows[:, piece * width : (piece + 1) * width],
-                )
+            first = tile * IN_FEATURES
+            nc.sync.dma_start(
+                out=out_dram[span, :, first : first + PAIR * IN_FEATURES], in_=out_rows[:]
+            )
+
+        def multiply_first_pair(out_rows, operand, half):
+            for r in range(PAIR):
+                one_pass(out_rows, operand, r, half, on_vector=(r == 1))
+            cols = slice(half * N_PASS, (half + 1) * N_PASS)
+            nc.sync.dma_start(
+                out=out_dram[0].rearrange("p (i n) -> p i n", n=IN_FEATURES)[:, :PAIR, cols],
+                in_=out_rows[:].rearrange("p (r n) -> p r n", r=PAIR)[:, :, cols],
+            )
 
         pairs = TOKEN_TILES // PAIR
         with tc.manual_schedule(engines={mybir.EngineType.PE}):
@@ -186,14 +194,21 @@ def tile_quaternionlinear_t_kernel(
             idle_matmuls(KEEP_WARM)
             for c in range(BLOCK_ROWS):
                 prepare_w(c)
-                idle_matmuls(KEEP_WARM)
-            quantised = {0: quantise(grouped[0])}
+                if c == 1:
+                    quantised = {0: quantise(grouped[0])}
+                if c + 1 < BLOCK_ROWS:
+                    idle_matmuls(KEEP_WARM)
+            first_rows = results.tile([P, PAIR * IN_FEATURES], F32, tag="out_rows")
             grouped[1] = regroup(1)
-        for s in range(pairs):
+            multiply_first_pair(first_rows, quantised[0], 0)
+            grouped[2] = regroup(2)
+            quantised[1] = quantise(grouped[1])
+            multiply_first_pair(first_rows, quantised[0], 1)
+        for s in range(1, pairs):
             if s + 1 < pairs:
                 quantised[s + 1] = quantise(grouped[s + 1])
-            multiply(s, quantised[s][0], quantised[s][1])
-            if s == 0:
-                grouped[2] = regroup(2)
+            multiply(s, quantised[s])
+            if s == 1:
+                grouped[3] = regroup(3)
             if s + 3 < pairs:
                 grouped[s + 3] = regroup(s + 3)

@@ -23,8 +23,8 @@ CHUNKS = (2, 2, 4, 8, 8, 8)
 assert sum(CHUNKS) == TOKEN_TILES and all(size % PAIR == 0 for size in CHUNKS)
 assert sum(CHUNKS[:3]) == SPAN_TILES and all(size == SPAN_TILES for size in CHUNKS[3:])
 WORDS = K // 2
-WARM_UP = 20
-KEEP_WARM = 4
+WARM_UP = 5
+KEEP_WARM = 1
 
 HAMILTON = (
     ((+1.0, 0), (+1.0, 1), (+1.0, 2), (+1.0, 3)),
@@ -87,8 +87,8 @@ def tile_quaternionlinear_t_kernel(
                         in_=matrix.rearrange("(h n) k -> n h k", n=P),
                     )
 
-        zeros = constants.tile([P, P], BF16)
-        nc.gpsimd.memset(zeros[:], 0.0)
+        zeros = constants.tile([P, N_PASS], BF16)
+        nc.vector.memset(zeros[:], 0.0)
         identity = constants.tile([P, P], F32)
         make_identity(nc, identity[:])
 
@@ -97,7 +97,7 @@ def tile_quaternionlinear_t_kernel(
         def idle_matmuls(count):
             for w in range(count):
                 nc.tensor.matmul(
-                    out=idle_sum[:, :P], lhsT=zeros[:], rhs=zeros[:], start=True, stop=True
+                    out=idle_sum[:], lhsT=zeros[:, :P], rhs=zeros[:], start=True, stop=True
                 )
 
         w_grouped = constants.tile([P, IN_FEATURES * PACK], BF16, align_bytes=64)

import concourse.mybir as mybir
from concourse.masks import make_identity

F32 = mybir.dt.float32
BF16 = mybir.dt.bfloat16
U32 = mybir.dt.uint32
U8 = mybir.dt.uint8
E4M3_X4 = mybir.dt.float8_e4m3fn_x4
E5M2_X4 = mybir.dt.float8_e5m2_x4

P = 128
PACK = 4
K = P * PACK
N_PASS = 512

TOKENS, IN_FEATURES, OUT_FEATURES = 4096, 1024, 512
assert OUT_FEATURES == K

TOKEN_TILES = TOKENS // P
SPAN_TILES = 8
PAIR = 2
CHUNKS = (2, 2, 4, 8, 8, 8)
assert sum(CHUNKS) == TOKEN_TILES and all(size % PAIR == 0 for size in CHUNKS)
assert sum(CHUNKS[:3]) == SPAN_TILES and all(size == SPAN_TILES for size in CHUNKS[3:])
WORDS = K // 2
WARM_UP = 5
KEEP_WARM = 1

HAMILTON = (
    ((+1.0, 0), (+1.0, 1), (+1.0, 2), (+1.0, 3)),
    ((-1.0, 1), (+1.0, 0), (+1.0, 3), (-1.0, 2)),
    ((-1.0, 2), (-1.0, 3), (+1.0, 0), (+1.0, 1)),
    ((-1.0, 3), (+1.0, 2), (-1.0, 1), (+1.0, 0)),
)
BLOCK_ROWS = 4
BLOCK_K = OUT_FEATURES // 4
HALVES = IN_FEATURES // 4 // P
assert HALVES == PAIR

FLOPS = 2 * TOKENS * IN_FEATURES * OUT_FEATURES
BYTES = 2 * TOKENS * OUT_FEATURES + 2 * IN_FEATURES * BLOCK_K + 4 * TOKENS * IN_FEATURES


def pair_to_k_major(nc, banks, identity, row_words, grouped_words):
    bank = banks.tile([P, PAIR, 2, P], F32)
    for r in range(PAIR):
        for u in range(2):
            nc.tensor.transpose(bank[:, r, u, :], row_words[:, r, u, :], identity)
    nc.scalar.copy(out=grouped_words, in_=bank[:].rearrange("p r u n -> p r n u"))


def tile_quaternionlinear_t_kernel(
    tc, x, Wr, Wi, Wj, Wk, br, bi, bj, bk, grad_out, out
):
    nc = tc.nc
    g_dram = grad_out.rearrange("(b p i) k -> b p (i k)", p=P, i=SPAN_TILES)
    out_dram = out.rearrange("(b p i) n -> b p (i n)", p=P, i=SPAN_TILES)

    with (
        tc.tile_pool(name="constants", bufs=1) as constants,
        tc.tile_pool(name="loads", bufs=1) as loads,
        tc.tile_pool(name="operands", bufs=4) as operands,
        tc.tile_pool(name="results", bufs=8) as results,
        tc.psum_pool(name="banks", bufs=2) as banks,
        tc.psum_pool(name="sums", bufs=6) as sums,
    ):
        w_rows = constants.tile([P, BLOCK_ROWS * PAIR * K], BF16)
        w_blocks = w_rows[:].rearrange(
            "n (c h j k) -> n c h j k", c=BLOCK_ROWS, h=PAIR, j=4
        )
        g_pairs = []
        for d, size in enumerate(CHUNKS):
            g_rows = loads.tile([P, size * K], BF16, name="g_rows%d" % d)
            span, tile = divmod(len(g_pairs) * PAIR, SPAN_TILES)
            nc.sync.dma_start(
                out=g_rows[:], in_=g_dram[span, :, tile * K : (tile + size) * K]
            )
            g_row_words = g_rows[:].bitcast(F32).rearrange(
                "n (i p u) -> n i u p", i=size, u=2
            )
            for i in range(0, size, PAIR):
                g_pairs.append(g_row_words[:, i : i + PAIR])
            if d == 0:
                for m, matrix in enumerate((Wr, Wi, Wj, Wk)):
                    nc.sync.dma_start(
                        out=w_blocks[:, 0, :, m, :],
                        in_=matrix.rearrange("(h n) k -> n h k", n=P),
                    )

        zeros = constants.tile([P, N_PASS], BF16)
        nc.vector.memset(zeros[:], 0.0)
        identity = constants.tile([P, P], F32)
        make_identity(nc, identity[:])

        idle_sum = sums.tile([P, N_PASS], F32, tag="acc")

        def idle_matmuls(count):
            for w in range(count):
                nc.tensor.matmul(
                    out=idle_sum[:], lhsT=zeros[:, :P], rhs=zeros[:], start=True, stop=True
                )

        w_grouped = constants.tile([P, IN_FEATURES * PACK], BF16, align_bytes=64)
        w_codes = constants.tile([P, IN_FEATURES], U32, align_bytes=64)
        w_scales = constants.tile([P, IN_FEATURES], U8, align_bytes=64)
        w_row_words = w_rows[:].bitcast(F32).rearrange(
            "n (c h p u) -> n c h u p", c=BLOCK_ROWS, h=PAIR, u=2
        )
        w_grouped_words = w_grouped[:].bitcast(F32).rearrange(
            "p (c h n u) -> p c h n u", c=BLOCK_ROWS, h=PAIR, u=2
        )

        def prepare_w(c):
            if c > 0:
                for j, (sign, m) in enumerate(HAMILTON[c]):
                    nc.vector.tensor_scalar_mul(
                        out=w_blocks[:, c, :, j, :],
                        in0=w_blocks[:, 0, :, m, :],
                        scalar1=sign,
                    )
            pair_to_k_major(
                nc, banks, identity[:], w_row_words[:, c], w_grouped_words[:, c]
            )
            rows = slice(c * PAIR * P, (c + 1) * PAIR * P)
            nc.vector.quantize_mx(
                out=w_codes[:, rows].bitcast(E4M3_X4),
                scales=w_scales[:, rows],
                in_=w_grouped[:, c * PAIR * P * PACK : (c + 1) * PAIR * P * PACK],
            )

        def regroup(s):
            g_grouped = operands.tile([P, PAIR * P * PACK], BF16, align_bytes=64)
            pair_to_k_major(
                nc,
                banks,
                identity[:],
                g_pairs[s],
                g_grouped[:].bitcast(F32).rearrange("p (r n u) -> p r n u", r=PAIR, u=2),
            )
            return g_grouped

        def quantise(g_grouped):
            g_codes = operands.tile([P, PAIR * P], U32, align_bytes=64)
            g_scales = operands.tile([P, PAIR * P], U8, align_bytes=64)
            nc.vector.quantize_mx(
                out=g_codes[:].bitcast(E5M2_X4), scales=g_scales[:], in_=g_grouped[:]
            )
            return g_codes, g_scales

        def one_pass(out_rows, operand, r, half, on_vector):
            g_codes, g_scales = operand
            tokens = slice(r * P, (r + 1) * P)
            cols = slice(half * N_PASS, (half + 1) * N_PASS)
            acc = sums.tile([P, N_PASS], F32, tag="acc")
            nc.tensor.matmul_mx(
                out=acc[:],
                lhsT=g_codes[:, tokens].bitcast(E5M2_X4),
                lhsT_scale=g_scales[:, tokens],
                rhs=w_codes[:, cols].bitcast(E4M3_X4),
                rhs_scale=w_scales[:, cols],
                start=True,
                stop=True,
            )
            first = r * IN_FEATURES + half * N_PASS
            if on_vector:
                nc.vector.tensor_copy(out=out_rows[:, first : first + N_PASS], in_=acc[:])
            else:
                nc.scalar.copy(out=out_rows[:, first : first + N_PASS], in_=acc[:])

        def multiply(s, operand):
            out_rows = results.tile([P, PAIR * IN_FEATURES], F32, tag="out_rows")
            for r in range(PAIR):
                for half in range(IN_FEATURES // N_PASS):
                    one_pass(out_rows, operand, r, half, on_vector=(half == 1))
            span, tile = divmod(s * PAIR, SPAN_TILES)
            first = tile * IN_FEATURES
            nc.sync.dma_start(
                out=out_dram[span, :, first : first + PAIR * IN_FEATURES], in_=out_rows[:]
            )

        def multiply_first_pair(out_rows, operand, half):
            for r in range(PAIR):
                one_pass(out_rows, operand, r, half, on_vector=(r == 1))
            cols = slice(half * N_PASS, (half + 1) * N_PASS)
            nc.sync.dma_start(
                out=out_dram[0].rearrange("p (i n) -> p i n", n=IN_FEATURES)[:, :PAIR, cols],
                in_=out_rows[:].rearrange("p (r n) -> p r n", r=PAIR)[:, :, cols],
            )

        pairs = TOKEN_TILES // PAIR
        with tc.manual_schedule(engines={mybir.EngineType.PE}):
            idle_matmuls(WARM_UP)
            grouped = {0: regroup(0)}
            idle_matmuls(KEEP_WARM)
            for c in range(BLOCK_ROWS):
                prepare_w(c)
                if c == 1:
                    quantised = {0: quantise(grouped[0])}
                if c + 1 < BLOCK_ROWS:
                    idle_matmuls(KEEP_WARM)
            first_rows = results.tile([P, PAIR * IN_FEATURES], F32, tag="out_rows")
            grouped[1] = regroup(1)
            multiply_first_pair(first_rows, quantised[0], 0)
            grouped[2] = regroup(2)
            quantised[1] = quantise(grouped[1])
            multiply_first_pair(first_rows, quantised[0], 1)
        for s in range(1, pairs):
            if s + 1 < pairs:
                quantised[s + 1] = quantise(grouped[s + 1])
            multiply(s, quantised[s])
            if s == 1:
                grouped[3] = regroup(3)
            if s + 3 < pairs:
                grouped[s + 3] = regroup(s + 3)
